import numpy as np
import ml_dtypes


def mxq(x, axis, fmt="e4m3"):
    dtype, down = {"e4m3": (ml_dtypes.float8_e4m3fn, 7), "e5m2": (ml_dtypes.float8_e5m2, 14)}[fmt]
    v = np.moveaxis(np.asarray(x, np.float32).astype(ml_dtypes.bfloat16).astype(np.float64), axis, -1)
    blocks = v.reshape(v.shape[:-1] + (-1, 32))
    amax = np.abs(blocks).max(-1, keepdims=True)
    byte = np.maximum(np.where(amax > 0, np.frexp(amax)[1] - 1 + 127, 0) - down, 1)
    scale = np.exp2(byte - 127.0)
    codes = (blocks / scale).astype(np.float32).astype(dtype).astype(np.float64)
    return np.moveaxis((codes * scale).reshape(v.shape), -1, axis)


WIDE = False


def mx_kscale(k):
    if not WIDE:
        return np.ones(k)
    levels = np.array([10, -10, 5, -5, 0])
    a = np.random.permutation(np.resize(levels, k // 512 * 4)).reshape(k // 512, 4)
    idx = np.arange(k)
    return np.exp2(a[idx // 512, idx % 128 // 32])


BF16 = ml_dtypes.bfloat16


def bf(x):
    return np.asarray(x, np.float32).astype(BF16)


def f64(x):
    return np.asarray(x).astype(np.float64)


E2M1 = np.array([0.0, 0.5, 1.0, 1.5, 2.0, 3.0, 4.0, 6.0, -0.0, -0.5, -1.0, -1.5, -2.0, -3.0, -4.0, -6.0])


def pack_weight(w, fmt):
    k, n = w.shape
    w = f64(bf(w)).reshape(k // 32, 32, n)
    amax = np.abs(w).max(1)
    if fmt == "e4m3":
        byte = np.frexp(amax)[1] - 1 + 127 - 7
    else:
        mant, ex = np.frexp(amax / 6.0)
        byte = np.where(mant > 0.5, ex, ex - 1) + 127
    byte = np.clip(np.where(amax > 0, byte, 1), 1, 254)
    scaled = (w * np.exp2(127.0 - byte)[:, None, :]).reshape(k, n).astype(np.float32)
    by_word = np.ascontiguousarray(scaled.reshape(k // 512, 128, 4, n).transpose(0, 1, 3, 2))
    if fmt == "e4m3":
        words = by_word.astype(ml_dtypes.float8_e4m3fn).view(np.uint8)
    else:
        c = by_word.astype(ml_dtypes.float4_e2m1fn).view(np.uint8) & 0xF
        words = c[..., 0::2] | (c[..., 1::2] << 4)
    return np.ascontiguousarray(words), np.ascontiguousarray(byte.astype(np.uint8).reshape(k // 512, 16, n))


def unpack_weight(words, scales, fmt):
    g, p, n, _ = words.shape
    if fmt == "e4m3":
        vals = np.ascontiguousarray(words).view(ml_dtypes.float8_e4m3fn).astype(np.float64)
    else:
        nib = np.empty((g, p, n, 4), np.uint8)
        nib[..., 0::2] = words & 0xF
        nib[..., 1::2] = words >> 4
        vals = E2M1[nib]
    vals = vals * np.repeat(np.exp2(scales.astype(np.float64) - 127.0), 8, axis=1)[..., None]
    return vals.transpose(0, 1, 3, 2).reshape(g * 512, n)


N, D, H = 8192, 1024, 256
H2 = H + H
LN_EPS = 1e-5
ERF_TERMS = 120
FMT = "e4m3"


def erf(x):
    a = np.clip(x, -6.0, 6.0)
    term = a
    total = a
    for n in range(1, ERF_TERMS):
        term = term * (2.0 * a * a / (2.0 * n + 1.0))
        total = total + term
    return 2.0 / np.sqrt(np.pi) * np.exp(-a * a) * total


def gelu(v):
    return 0.5 * v * (1.0 + erf(v / np.sqrt(2.0)))


def layernorm(x, g, b):
    m = x.mean(-1, keepdims=True)
    v = np.square(x - m).mean(-1, keepdims=True)
    return (x - m) / np.sqrt(v + LN_EPS) * g + b


def setup_inputs():
    s, t = mx_kscale(D), mx_kscale(H2)
    z = bf(np.random.standard_normal((N, D)) * s)
    attention_out = bf(np.random.standard_normal((N, H)) * t[H:])
    Wz_words, Wz_scales = pack_weight(np.ascontiguousarray((np.random.standard_normal((H, D)) / np.sqrt(D) / s).T), FMT)
    bz = bf(0.1 * np.random.standard_normal(H))
    gz = bf((1.0 + 0.1 * np.random.standard_normal(H)) * t[:H])
    bz_ln = bf(0.1 * np.random.standard_normal(H) * t[:H])
    w1_deq_words, w1_deq_scales = pack_weight(np.ascontiguousarray((np.random.standard_normal((H, H2)) / np.sqrt(H2) / t).T), FMT)
    b1 = bf(0.1 * np.random.standard_normal(H))
    g1 = bf(1.0 + 0.1 * np.random.standard_normal(H))
    b1_ln = bf(0.1 * np.random.standard_normal(H))
    return {
        "z": z,
        "attention_out": attention_out,
        "Wz_words": Wz_words,
        "Wz_scales": Wz_scales,
        "bz": bz,
        "gz": gz,
        "bz_ln": bz_ln,
        "w1_deq_words": w1_deq_words,
        "w1_deq_scales": w1_deq_scales,
        "b1": b1,
        "g1": g1,
        "b1_ln": b1_ln,
    }


def reference(z, attention_out, Wz_words, Wz_scales, bz, gz, bz_ln, w1_deq_words, w1_deq_scales, b1, g1, b1_ln):
    z_proj = layernorm((mxq(f64(z), 1, "e4m3") @ unpack_weight(Wz_words, Wz_scales, FMT)) + f64(bz), f64(gz), f64(bz_ln))
    combined = np.concatenate([z_proj, f64(attention_out)], axis=-1)
    y = (mxq(combined, 1, "e4m3") @ unpack_weight(w1_deq_words, w1_deq_scales, FMT)) + f64(b1)
    return gelu(layernorm(y, f64(g1), f64(b1_ln)))

@@ -1,0 +1,274 @@
+from contextlib import ExitStack
+
+import concourse.mybir as mybir
+from concourse.masks import make_identity
+
+F32 = mybir.dt.float32
+BF16 = mybir.dt.bfloat16
+I32 = mybir.dt.int32
+U32 = mybir.dt.uint32
+U8 = mybir.dt.uint8
+FP8X4 = mybir.dt.float8_e4m3fn_x4
+ALU = mybir.AluOpType
+ACT = mybir.ActivationFunctionType
+
+P = 128
+PACK = 4
+K_PASS = P * PACK
+WORDS = K_PASS // 2
+N_TOKENS, D, H = 8192, 1024, 256
+Z_PASSES = D // K_PASS
+LN_EPS = 1e-5
+PAIR = 2
+UNITS = N_TOKENS // (P * PAIR)
+LOAD_AHEAD = 3
+LAST_LAG = 10
+
+FLOPS = 2 * N_TOKENS * D * H + 2 * N_TOKENS * (2 * H) * H
+
+
+def load_weight(nc, const, words, scales, passes, name):
+    codes = const.tile([P, passes, H], U32, name=name + "_codes", align_bytes=64)
+    nc.sync.dma_start(
+        out=codes[:].bitcast(I32),
+        in_=words.rearrange("g p n t -> p g (n t)").bitcast(I32),
+    )
+    plane = const.tile([P, passes, H], U8, name=name + "_scales", align_bytes=64)
+    nc.vector.memset(plane[:].bitcast(I32), 0)
+    for quadrant in range(4):
+        nc.sync.dma_start(
+            out=plane[32 * quadrant : 32 * quadrant + 4].bitcast(I32),
+            in_=scales[:, 4 * quadrant : 4 * quadrant + 4, :].rearrange("g r n -> r g n").bitcast(I32),
+        )
+    return codes, plane
+
+
+def load_row(nc, const, vector, name):
+    row = const.tile([P, H], BF16, name=name)
+    nc.scalar.dma_start(out=row[:], in_=vector.partition_broadcast(P))
+    return row
+
+
+def transpose_words(nc, bank, token_words, identity):
+    for u in range(2):
+        nc.tensor.transpose(bank[:, u, :], token_words[:, u:WORDS:2], identity[:])
+
+
+def tile_synapsemodel_pa_t_kernel(
+    tc, z, attention_out, Wz_words, Wz_scales, bz, gz, bz_ln, w1_deq_words, w1_deq_scales, b1, g1, b1_ln, out
+):
+    nc = tc.nc
+    z_units = z.rearrange("(u p i) d -> u p i d", p=P, i=PAIR)
+    attention_units = attention_out.rearrange("(u p i) h -> u p i h", p=P, i=PAIR)
+    out_units = out.rearrange("(u p i) h -> u p i h", p=P, i=PAIR)
+
+    with ExitStack() as stack:
+        const = stack.enter_context(tc.tile_pool(name="const", bufs=1))
+        brief = stack.enter_context(tc.tile_pool(name="brief", bufs=3))
+        lasting = stack.enter_context(tc.tile_pool(name="lasting", bufs=5))
+        longest = stack.enter_context(tc.tile_pool(name="longest", bufs=10))
+        psum = stack.enter_context(tc.psum_pool(name="psum", bufs=2))
+
+        held = {}
+
+        def load(u):
+            z_rows = lasting.tile([P, PAIR, D], BF16, name="z_rows")
+            nc.sync.dma_start(out=z_rows[:], in_=z_units[u])
+            combined = longest.tile([P, PAIR, 2 * H], BF16, name="combined")
+            nc.sync.dma_start(out=combined[:, :, H : 2 * H], in_=attention_units[u])
+            held["z_rows", u] = z_rows
+            held["combined", u] = combined
+
+        stack.enter_context(tc.manual_schedule())
+
+        load(0)
+        wz_codes, wz_scales = load_weight(nc, const, Wz_words, Wz_scales, Z_PASSES, "wz")
+        w1_codes, w1_scales = load_weight(nc, const, w1_deq_words, w1_deq_scales, 1, "w1")
+        bias_row = {1: load_row(nc, const, bz, "bz_row"), 2: load_row(nc, const, b1, "b1_row")}
+        gain_row = {1: load_row(nc, const, gz, "gz_row"), 2: load_row(nc, const, g1, "g1_row")}
+        shift_row = {1: load_row(nc, const, bz_ln, "bz_ln_row"), 2: load_row(nc, const, b1_ln, "b1_ln_row")}
+        identity = const.tile([P, P], F32)
+        make_identity(nc, identity[:])
+        minus_half = const.tile([P, PAIR], F32)
+        nc.vector.memset(minus_half[:], -0.5)
+        for u in range(1, LOAD_AHEAD):
+            load(u)
+
+        def transpose_z(u):
+            z_words = held["z_rows", u][:].bitcast(F32)
+            z_grouped = brief.tile([P, PAIR, Z_PASSES, P, PACK], BF16, name="z_grouped", align_bytes=64)
+            for i in range(PAIR):
+                z_bank = psum.tile([P, Z_PASSES, 2, P], F32, name="z_bank")
+                for g in range(Z_PASSES):
+                    transpose_words(nc, z_bank[:, g], z_words[:, i, WORDS * g : WORDS * (g + 1)], identity)
+                nc.scalar.copy(out=z_grouped[:, i].bitcast(F32), in_=z_bank[:].rearrange("p g u r -> p g r u"))
+            held["z_grouped", u] = z_grouped
+
+        def quantise_z(u):
+            z_codes = brief.tile([P, PAIR, Z_PASSES, P], U32, name="z_codes", align_bytes=64)
+            z_scales = brief.tile([P, PAIR, Z_PASSES, P], U8, name="z_scales", align_bytes=64)
+            nc.vector.quantize_mx(
+                out=z_codes[:].rearrange("p i g r -> p (i g r)").bitcast(FP8X4),
+                scales=z_scales[:].rearrange("p i g r -> p (i g r)"),
+                in_=held["z_grouped", u][:].rearrange("p i g r t -> p (i g r t)"),
+            )
+            held["z_codes", u] = z_codes
+            held["z_scales", u] = z_scales
+
+        def multiply_z(u):
+            z_codes, z_scales = held["z_codes", u], held["z_scales", u]
+            y_bank = psum.tile([P, PAIR, H], F32, name="y1_bank")
+            for i in range(PAIR):
+                for g in range(Z_PASSES):
+                    nc.tensor.matmul_mx(
+                        out=y_bank[:, i, :],
+                        lhsT=z_codes[:, i, g, :].bitcast(FP8X4),
+                        lhsT_scale=z_scales[:, i, g, :],
+                        rhs=wz_codes[:, g, :].bitcast(FP8X4),
+                        rhs_scale=wz_scales[:, g, :],
+                        start=(g == 0),
+                        stop=(g == Z_PASSES - 1),
+                    )
+            held["y_bank", 1, u] = y_bank
+
+        def add_bias(layer, u):
+            y_bank = held["y_bank", layer, u]
+            x = lasting.tile([P, PAIR, H], F32, name="x%d" % layer)
+            row_sum = lasting.tile([P, PAIR], F32, name="row_sum%d" % layer)
+            for i in range(PAIR):
+                nc.vector.scalar_tensor_tensor(
+                    out=x[:, i, :],
+                    in0=y_bank[:, i, :],
+                    scalar=1.0,
+                    in1=bias_row[layer][:],
+                    op0=ALU.mult,
+                    op1=ALU.add,
+                    accum_out=row_sum[:, i : i + 1],
+                )
+            held["x", layer, u] = x
+            held["row_sum", layer, u] = row_sum
+
+        def means(layer, u):
+            neg_mean = lasting.tile([P, PAIR], F32, name="neg_mean%d" % layer)
+            nc.scalar.mul(out=neg_mean[:], in_=held["row_sum", layer, u][:], mul=-1.0 / H)
+            held["neg_mean", layer, u] = neg_mean
+
+        def sum_squares(layer, u):
+            x, neg_mean = held["x", layer, u], held["neg_mean", layer, u]
+            square_sum = lasting.tile([P, PAIR], F32, name="square_sum%d" % layer)
+            for i in range(PAIR):
+                squares = lasting.tile([P, H], BF16, name="squares")
+                nc.scalar.activation(
+                    out=squares[:],
+                    in_=x[:, i, :],
+                    func=ACT.Square,
+                    bias=neg_mean[:, i : i + 1],
+                    scale=1.0,
+                    accum_out=square_sum[:, i : i + 1],
+                )
+            held["square_sum", layer, u] = square_sum
+
+        def deviations(layer, u):
+            variance_eps = lasting.tile([P, PAIR], F32, name="variance_eps%d" % layer)
+            nc.scalar.activation(
+                out=variance_eps[:], in_=held["square_sum", layer, u][:], func=ACT.Copy, bias=LN_EPS, scale=1.0 / H
+            )
+            rstd = lasting.tile([P, PAIR], F32, name="rstd%d" % layer)
+            nc.gpsimd.tensor_tensor(out=rstd[:], in0=variance_eps[:], in1=minus_half[:], op=ALU.pow)
+            held["rstd", layer, u] = rstd
+
+        def centre(layer, u):
+            x, neg_mean = held["x", layer, u], held["neg_mean", layer, u]
+            centred = brief.tile([P, PAIR, H], F32, name="centred%d" % layer)
+            for i in range(PAIR):
+                nc.vector.scalar_tensor_tensor(
+                    out=centred[:, i, :], in0=x[:, i, :], scalar=neg_mean[:, i : i + 1], in1=gain_row[layer][:],
+                    op0=ALU.add, op1=ALU.mult,
+                )
+            held["centred", layer, u] = centred
+
+        def rescale(layer, u, result):
+            centred, rstd = held["centred", layer, u], held["rstd", layer, u]
+            for i in range(PAIR):
+                nc.vector.scalar_tensor_tensor(
+                    out=result[:, i, :], in0=centred[:, i, :], scalar=rstd[:, i : i + 1], in1=shift_row[layer][:],
+                    op0=ALU.mult, op1=ALU.add,
+                )
+
+        def project(u):
+            rescale(1, u, held["combined", u][:, :, 0:H])
+
+        def transpose_combined(u):
+            combined_words = held["combined", u][:].bitcast(F32)
+            c_bank = psum.tile([P, PAIR, 2, P], F32, name="c_bank")
+            for i in range(PAIR):
+                transpose_words(nc, c_bank[:, i], combined_words[:, i, :], identity)
+            c_grouped = brief.tile([P, PAIR, P, PACK], BF16, name="c_grouped", align_bytes=64)
+            nc.scalar.copy(out=c_grouped[:].bitcast(F32), in_=c_bank[:].rearrange("p i u r -> p i r u"))
+            held["c_grouped", u] = c_grouped
+
+        def quantise_combined(u):
+            c_codes = brief.tile([P, PAIR, P], U32, name="c_codes", align_bytes=64)
+            c_scales = brief.tile([P, PAIR, P], U8, name="c_scales", align_bytes=64)
+            nc.vector.quantize_mx(
+                out=c_codes[:].rearrange("p i r -> p (i r)").bitcast(FP8X4),
+                scales=c_scales[:].rearrange("p i r -> p (i r)"),
+                in_=held["c_grouped", u][:].rearrange("p i r t -> p (i r t)"),
+            )
+            held["c_codes", u] = c_codes
+            held["c_scales", u] = c_scales
+
+        def multiply_combined(u):
+            c_codes, c_scales = held["c_codes", u], held["c_scales", u]
+            y_bank = psum.tile([P, PAIR, H], F32, name="y2_bank")
+            for i in range(PAIR):
+                nc.tensor.matmul_mx(
+                    out=y_bank[:, i, :],
+                    lhsT=c_codes[:, i, :].bitcast(FP8X4),
+                    lhsT_scale=c_scales[:, i, :],
+                    rhs=w1_codes[:, 0, :].bitcast(FP8X4),
+                    rhs_scale=w1_scales[:, 0, :],
+                    start=True,
+                    stop=True,
+                )
+            held["y_bank", 2, u] = y_bank
+
+        def normalise_output(u):
+            normed = brief.tile([P, PAIR, H], F32, name="normed")
+            rescale(2, u, normed)
+            held["normed", u] = normed
+
+        def gelu_and_store(u):
+            result = brief.tile([P, PAIR, H], F32, name="result")
+            nc.scalar.activation(
+                out=result[:].rearrange("p i h -> p (i h)"),
+                in_=held["normed", u][:].rearrange("p i h -> p (i h)"),
+                func=ACT.Gelu,
+            )
+            nc.scalar.dma_start(out=out_units[u], in_=result[:])
+
+        def run(stage, *unit):
+            if 0 <= unit[-1] < UNITS:
+                stage(*unit)
+
+        for s in range(UNITS + LAST_LAG + 1):
+            run(load, s + LOAD_AHEAD)
+            run(multiply_z, s - 2)
+            run(multiply_combined, s - 7)
+            run(add_bias, 1, s - 2)
+            run(add_bias, 2, s - 7)
+            run(means, 1, s - 3)
+            run(means, 2, s - 8)
+            run(gelu_and_store, s - LAST_LAG)
+            run(sum_squares, 1, s - 3)
+            run(sum_squares, 2, s - 8)
+            run(centre, 1, s - 4)
+            run(centre, 2, s - 9)
+            run(quantise_z, s - 1)
+            run(quantise_combined, s - 6)
+            run(project, s - 4)
+            run(normalise_output, s - 9)
+            run(transpose_combined, s - 5)
+            run(deviations, 1, s - 3)
+            run(deviations, 2, s - 8)
+            run(transpose_z, s)

@@ -23,6 +23,7 @@ PAIR = 2
 UNITS = N_TOKENS // (P * PAIR)
 LOAD_AHEAD = 3
 LAST_LAG = 10
+BIAS_LAG = {1: 2, 2: 7}
 
 FLOPS = 2 * N_TOKENS * D * H + 2 * N_TOKENS * (2 * H) * H
 
@@ -89,7 +90,7 @@ def tile_synapsemodel_pa_t_kernel(
         shift_row = {1: load_row(nc, const, bz_ln, "bz_ln_row"), 2: load_row(nc, const, b1_ln, "b1_ln_row")}
         identity = const.tile([P, P], F32)
         make_identity(nc, identity[:])
-        minus_half = const.tile([P, PAIR], F32)
+        minus_half = const.tile([P, 2, PAIR], F32)
         nc.vector.memset(minus_half[:], -0.5)
         for u in range(1, LOAD_AHEAD):
             load(u)
@@ -131,10 +132,16 @@ def tile_synapsemodel_pa_t_kernel(
                     )
             held["y_bank", 1, u] = y_bank
 
+        def layers_of_step(t):
+            live = [layer - 1 for layer in (1, 2) if 0 <= t - BIAS_LAG[layer] < UNITS]
+            return slice(live[0], live[-1] + 1) if live else None
+
         def add_bias(layer, u):
+            t = u + BIAS_LAG[layer]
+            if ("row_sum", t) not in held:
+                held["row_sum", t] = lasting.tile([P, 2, PAIR], F32, name="row_sum")
             y_bank = held["y_bank", layer, u]
             x = lasting.tile([P, PAIR, H], F32, name="x%d" % layer)
-            row_sum = lasting.tile([P, PAIR], F32, name="row_sum%d" % layer)
             for i in range(PAIR):
                 nc.vector.scalar_tensor_tensor(
                     out=x[:, i, :],
@@ -143,55 +150,62 @@ def tile_synapsemodel_pa_t_kernel(
                     in1=bias_row[layer][:],
                     op0=ALU.mult,
                     op1=ALU.add,
-                    accum_out=row_sum[:, i : i + 1],
+                    accum_out=held["row_sum", t][:, layer - 1, i : i + 1],
                 )
             held["x", layer, u] = x
-            held["row_sum", layer, u] = row_sum
 
-        def means(layer, u):
-            neg_mean = lasting.tile([P, PAIR], F32, name="neg_mean%d" % layer)
-            nc.scalar.mul(out=neg_mean[:], in_=held["row_sum", layer, u][:], mul=-1.0 / H)
-            held["neg_mean", layer, u] = neg_mean
+        def means(t):
+            layers = layers_of_step(t)
+            if layers is not None:
+                neg_mean = lasting.tile([P, 2, PAIR], F32, name="neg_mean")
+                nc.scalar.mul(out=neg_mean[:, layers], in_=held["row_sum", t][:, layers], mul=-1.0 / H)
+                held["neg_mean", t] = neg_mean
+                held["square_sum", t] = lasting.tile([P, 2, PAIR], F32, name="square_sum")
 
         def sum_squares(layer, u):
-            x, neg_mean = held["x", layer, u], held["neg_mean", layer, u]
-            square_sum = lasting.tile([P, PAIR], F32, name="square_sum%d" % layer)
+            t = u + BIAS_LAG[layer]
             for i in range(PAIR):
                 squares = lasting.tile([P, H], BF16, name="squares")
                 nc.scalar.activation(
                     out=squares[:],
-                    in_=x[:, i, :],
+                    in_=held["x", layer, u][:, i, :],
                     func=ACT.Square,
-                    bias=neg_mean[:, i : i + 1],
+                    bias=held["neg_mean", t][:, layer - 1, i : i + 1],
                     scale=1.0,
-                    accum_out=square_sum[:, i : i + 1],
+                    accum_out=held["square_sum", t][:, layer - 1, i : i + 1],
                 )
-            held["square_sum", layer, u] = square_sum
 
-        def deviations(layer, u):
-            variance_eps = lasting.tile([P, PAIR], F32, name="variance_eps%d" % layer)
-            nc.scalar.activation(
-                out=variance_eps[:], in_=held["square_sum", layer, u][:], func=ACT.Copy, bias=LN_EPS, scale=1.0 / H
-            )
-            rstd = lasting.tile([P, PAIR], F32, name="rstd%d" % layer)
-            nc.gpsimd.tensor_tensor(out=rstd[:], in0=variance_eps[:], in1=minus_half[:], op=ALU.pow)
-            held["rstd", layer, u] = rstd
+        def deviations(t):
+            layers = layers_of_step(t)
+            if layers is not None:
+                variance_eps = lasting.tile([P, 2, PAIR], F32, name="variance_eps")
+                nc.scalar.activation(
+                    out=variance_eps[:, layers], in_=held["square_sum", t][:, layers],
+                    func=ACT.Copy, bias=LN_EPS, scale=1.0 / H,
+                )
+                rstd = lasting.tile([P, 2, PAIR], F32, name="rstd")
+                nc.gpsimd.tensor_tensor(
+                    out=rstd[:, layers], in0=variance_eps[:, layers], in1=minus_half[:, layers], op=ALU.pow
+                )
+                held["rstd", t] = rstd
 
         def centre(layer, u):
-            x, neg_mean = held["x", layer, u], held["neg_mean", layer, u]
+            neg_mean = held["neg_mean", u + BIAS_LAG[layer]]
             centred = brief.tile([P, PAIR, H], F32, name="centred%d" % layer)
             for i in range(PAIR):
                 nc.vector.scalar_tensor_tensor(
-                    out=centred[:, i, :], in0=x[:, i, :], scalar=neg_mean[:, i : i + 1], in1=gain_row[layer][:],
+                    out=centred[:, i, :], in0=held["x", layer, u][:, i, :],
+                    scalar=neg_mean[:, layer - 1, i : i + 1], in1=gain_row[layer][:],
                     op0=ALU.add, op1=ALU.mult,
                 )
             held["centred", layer, u] = centred
 
         def rescale(layer, u, result):
-            centred, rstd = held["centred", layer, u], held["rstd", layer, u]
+            rstd = held["rstd", u + BIAS_LAG[layer]]
             for i in range(PAIR):
                 nc.vector.scalar_tensor_tensor(
-                    out=result[:, i, :], in0=centred[:, i, :], scalar=rstd[:, i : i + 1], in1=shift_row[layer][:],
+                    out=result[:, i, :], in0=held["centred", layer, u][:, i, :],
+                    scalar=rstd[:, layer - 1, i : i + 1], in1=shift_row[layer][:],
                     op0=ALU.mult, op1=ALU.add,
                 )
 
@@ -255,10 +269,9 @@ def tile_synapsemodel_pa_t_kernel(
             run(load, s + LOAD_AHEAD)
             run(multiply_z, s - 2)
             run(multiply_combined, s - 7)
-            run(add_bias, 1, s - 2)
-            run(add_bias, 2, s - 7)
-            run(means, 1, s - 3)
-            run(means, 2, s - 8)
+            run(add_bias, 1, s - BIAS_LAG[1])
+            run(add_bias, 2, s - BIAS_LAG[2])
+            means(s - 1)
             run(gelu_and_store, s - LAST_LAG)
             run(sum_squares, 1, s - 3)
             run(sum_squares, 2, s - 8)
@@ -269,6 +282,5 @@ def tile_synapsemodel_pa_t_kernel(
             run(project, s - 4)
             run(normalise_output, s - 9)
             run(transpose_combined, s - 5)
-            run(deviations, 1, s - 3)
-            run(deviations, 2, s - 8)
+            deviations(s - 1)
             run(transpose_z, s)

@@ -18,11 +18,12 @@ K_PASS = P * PACK
 WORDS = K_PASS // 2
 N_TOKENS, D, H = 8192, 1024, 256
 Z_PASSES = D // K_PASS
+HALVES = H // P
 LN_EPS = 1e-5
 PAIR = 2
 UNITS = N_TOKENS // (P * PAIR)
 LOAD_AHEAD = 3
-LAST_LAG = 10
+LAST_LAG = 11
 BIAS_LAG = {1: 2, 2: 7}
 
 FLOPS = 2 * N_TOKENS * D * H + 2 * N_TOKENS * (2 * H) * H
@@ -68,7 +69,7 @@ def tile_synapsemodel_pa_t_kernel(
         brief = stack.enter_context(tc.tile_pool(name="brief", bufs=3))
         lasting = stack.enter_context(tc.tile_pool(name="lasting", bufs=5))
         longest = stack.enter_context(tc.tile_pool(name="longest", bufs=10))
-        psum = stack.enter_context(tc.psum_pool(name="psum", bufs=2))
+        psum = stack.enter_context(tc.psum_pool(name="psum", bufs=1))
 
         held = {}
 
@@ -83,15 +84,27 @@ def tile_synapsemodel_pa_t_kernel(
         stack.enter_context(tc.manual_schedule())
 
         load(0)
+        identity = const.tile([P, P], F32)
+        make_identity(nc, identity[:])
+        vector_rows = const.tile([P, P], BF16)
+        nc.vector.memset(vector_rows[:], 0.0)
+        nc.scalar.dma_start(out=vector_rows[0:HALVES, :], in_=g1.rearrange("(h f) -> h f", h=HALVES))
+        nc.scalar.dma_start(out=vector_rows[HALVES : 2 * HALVES, :], in_=b1_ln.rearrange("(h f) -> h f", h=HALVES))
         wz_codes, wz_scales = load_weight(nc, const, Wz_words, Wz_scales, Z_PASSES, "wz")
         w1_codes, w1_scales = load_weight(nc, const, w1_deq_words, w1_deq_scales, 1, "w1")
         bias_row = {1: load_row(nc, const, bz, "bz_row"), 2: load_row(nc, const, b1, "b1_row")}
-        gain_row = {1: load_row(nc, const, gz, "gz_row"), 2: load_row(nc, const, g1, "g1_row")}
-        shift_row = {1: load_row(nc, const, bz_ln, "bz_ln_row"), 2: load_row(nc, const, b1_ln, "b1_ln_row")}
-        identity = const.tile([P, P], F32)
-        make_identity(nc, identity[:])
+        gz_row = load_row(nc, const, gz, "gz_row")
+        bz_ln_row = load_row(nc, const, bz_ln, "bz_ln_row")
         minus_half = const.tile([P, 2, PAIR], F32)
         nc.vector.memset(minus_half[:], -0.5)
+        vector_rows_f32 = const.tile([P, P], F32)
+        nc.vector.tensor_copy(out=vector_rows_f32[:], in_=vector_rows[:])
+        column_bank = psum.tile([P, P], F32)
+        nc.tensor.transpose(column_bank[:], vector_rows_f32[:], identity[:])
+        vector_columns = const.tile([P, 2 * HALVES], F32)
+        nc.vector.tensor_copy(out=vector_columns[:], in_=column_bank[:, 0 : 2 * HALVES])
+        g1_columns = vector_columns[:, 0:HALVES]
+        b1_ln_columns = vector_columns[:, HALVES : 2 * HALVES]
         for u in range(1, LOAD_AHEAD):
             load(u)
 
@@ -99,7 +112,7 @@ def tile_synapsemodel_pa_t_kernel(
             z_words = held["z_rows", u][:].bitcast(F32)
             z_grouped = brief.tile([P, PAIR, Z_PASSES, P, PACK], BF16, name="z_grouped", align_bytes=64)
             for i in range(PAIR):
-                z_bank = psum.tile([P, Z_PASSES, 2, P], F32, name="z_bank")
+                z_bank = psum.tile([P, Z_PASSES, 2, P], F32, name="z_bank", bufs=PAIR)
                 for g in range(Z_PASSES):
                     transpose_words(nc, z_bank[:, g], z_words[:, i, WORDS * g : WORDS * (g + 1)], identity)
                 nc.scalar.copy(out=z_grouped[:, i].bitcast(F32), in_=z_bank[:].rearrange("p g u r -> p g r u"))
@@ -189,28 +202,25 @@ def tile_synapsemodel_pa_t_kernel(
                 )
                 held["rstd", t] = rstd
 
-        def centre(layer, u):
-            neg_mean = held["neg_mean", u + BIAS_LAG[layer]]
-            centred = brief.tile([P, PAIR, H], F32, name="centred%d" % layer)
+        def centre(u):
+            neg_mean = held["neg_mean", u + BIAS_LAG[1]]
+            centred = brief.tile([P, PAIR, H], F32, name="centred")
             for i in range(PAIR):
                 nc.vector.scalar_tensor_tensor(
-                    out=centred[:, i, :], in0=held["x", layer, u][:, i, :],
-                    scalar=neg_mean[:, layer - 1, i : i + 1], in1=gain_row[layer][:],
+                    out=centred[:, i, :], in0=held["x", 1, u][:, i, :],
+                    scalar=neg_mean[:, 0, i : i + 1], in1=gz_row[:],
                     op0=ALU.add, op1=ALU.mult,
                 )
-            held["centred", layer, u] = centred
-
-        def rescale(layer, u, result):
-            rstd = held["rstd", u + BIAS_LAG[layer]]
-            for i in range(PAIR):
-                nc.vector.scalar_tensor_tensor(
-                    out=result[:, i, :], in0=held["centred", layer, u][:, i, :],
-                    scalar=rstd[:, layer - 1, i : i + 1], in1=shift_row[layer][:],
-                    op0=ALU.mult, op1=ALU.add,
-                )
+            held["centred", u] = centred
 
         def project(u):
-            rescale(1, u, held["combined", u][:, :, 0:H])
+            rstd = held["rstd", u + BIAS_LAG[1]]
+            for i in range(PAIR):
+                nc.vector.scalar_tensor_tensor(
+                    out=held["combined", u][:, i, 0:H], in0=held["centred", u][:, i, :],
+                    scalar=rstd[:, 0, i : i + 1], in1=bz_ln_row[:],
+                    op0=ALU.mult, op1=ALU.add,
+                )
 
         def transpose_combined(u):
             combined_words = held["combined", u][:].bitcast(F32)
@@ -247,19 +257,44 @@ def tile_synapsemodel_pa_t_kernel(
                 )
             held["y_bank", 2, u] = y_bank
 
-        def normalise_output(u):
+        def normalise(u):
+            t = u + BIAS_LAG[2]
             normed = brief.tile([P, PAIR, H], F32, name="normed")
-            rescale(2, u, normed)
+            for i in range(PAIR):
+                nc.vector.tensor_scalar(
+                    out=normed[:, i, :], in0=held["x", 2, u][:, i, :],
+                    scalar1=held["neg_mean", t][:, 1, i : i + 1], scalar2=held["rstd", t][:, 1, i : i + 1],
+                    op0=ALU.add, op1=ALU.mult,
+                )
             held["normed", u] = normed
 
-        def gelu_and_store(u):
+        def gelu_by_feature(u):
+            feature_bank = psum.tile([P, HALVES, PAIR, P], F32, name="feature_bank")
+            for h in range(HALVES):
+                for i in range(PAIR):
+                    nc.tensor.transpose(feature_bank[:, h, i, :], held["normed", u][:, i, P * h : P * (h + 1)], identity[:])
+            activated = brief.tile([P, HALVES, PAIR, P], F32, name="activated")
+            for h in range(HALVES):
+                nc.scalar.activation(
+                    out=activated[:, h].rearrange("p i r -> p (i r)"),
+                    in_=feature_bank[:, h].rearrange("p i r -> p (i r)"),
+                    func=ACT.Gelu,
+                    bias=b1_ln_columns[:, h : h + 1],
+                    scale=g1_columns[:, h : h + 1],
+                )
+            held["activated", u] = activated
+
+        def store_by_token(u):
+            token_bank = psum.tile([P, PAIR, H], F32, name="token_bank")
+            for i in range(PAIR):
+                for h in range(HALVES):
+                    nc.tensor.transpose(token_bank[:, i, P * h : P * (h + 1)], held["activated", u][:, h, i, :], identity[:])
             result = brief.tile([P, PAIR, H], F32, name="result")
-            nc.scalar.activation(
-                out=result[:].rearrange("p i h -> p (i h)"),
-                in_=held["normed", u][:].rearrange("p i h -> p (i h)"),
-                func=ACT.Gelu,
-            )
-            nc.scalar.dma_start(out=out_units[u], in_=result[:])
+            if u % 2 == 0:
+                nc.scalar.copy(out=result[:], in_=token_bank[:])
+            else:
+                nc.vector.tensor_copy(out=result[:], in_=token_bank[:])
+            nc.sync.dma_start(out=out_units[u], in_=result[:])
 
         def run(stage, *unit):
             if 0 <= unit[-1] < UNITS:
@@ -272,15 +307,15 @@ def tile_synapsemodel_pa_t_kernel(
             run(add_bias, 1, s - BIAS_LAG[1])
             run(add_bias, 2, s - BIAS_LAG[2])
             means(s - 1)
-            run(gelu_and_store, s - LAST_LAG)
+            run(transpose_combined, s - 5)
             run(sum_squares, 1, s - 3)
             run(sum_squares, 2, s - 8)
-            run(centre, 1, s - 4)
-            run(centre, 2, s - 9)
+            run(centre, s - 4)
             run(quantise_z, s - 1)
             run(quantise_combined, s - 6)
             run(project, s - 4)
-            run(normalise_output, s - 9)
-            run(transpose_combined, s - 5)
+            run(normalise, s - 9)
+            run(gelu_by_feature, s - 10)
             deviations(s - 1)
+            run(store_by_token, s - LAST_LAG)
             run(transpose_z, s)

@@ -23,8 +23,8 @@ LN_EPS = 1e-5
 PAIR = 2
 UNITS = N_TOKENS // (P * PAIR)
 LOAD_AHEAD = 3
-LAST_LAG = 11
-BIAS_LAG = {1: 2, 2: 7}
+LAST_LAG = 12
+BIAS_LAG = {1: 3, 2: 8}
 
 FLOPS = 2 * N_TOKENS * D * H + 2 * N_TOKENS * (2 * H) * H
 
@@ -68,7 +68,7 @@ def tile_synapsemodel_pa_t_kernel(
         const = stack.enter_context(tc.tile_pool(name="const", bufs=1))
         brief = stack.enter_context(tc.tile_pool(name="brief", bufs=3))
         lasting = stack.enter_context(tc.tile_pool(name="lasting", bufs=5))
-        longest = stack.enter_context(tc.tile_pool(name="longest", bufs=10))
+        longest = stack.enter_context(tc.tile_pool(name="longest", bufs=12))
         psum = stack.enter_context(tc.psum_pool(name="psum", bufs=1))
 
         held = {}
@@ -110,7 +110,7 @@ def tile_synapsemodel_pa_t_kernel(
 
         def transpose_z(u):
             z_words = held["z_rows", u][:].bitcast(F32)
-            z_grouped = brief.tile([P, PAIR, Z_PASSES, P, PACK], BF16, name="z_grouped", align_bytes=64)
+            z_grouped = lasting.tile([P, PAIR, Z_PASSES, P, PACK], BF16, name="z_grouped", align_bytes=64)
             for i in range(PAIR):
                 z_bank = psum.tile([P, Z_PASSES, 2, P], F32, name="z_bank", bufs=PAIR)
                 for g in range(Z_PASSES):
@@ -302,20 +302,20 @@ def tile_synapsemodel_pa_t_kernel(
 
         for s in range(UNITS + LAST_LAG + 1):
             run(load, s + LOAD_AHEAD)
-            run(multiply_z, s - 2)
-            run(multiply_combined, s - 7)
+            run(quantise_z, s - 2)
+            run(quantise_combined, s - 7)
+            run(multiply_z, s - 3)
+            run(multiply_combined, s - 8)
             run(add_bias, 1, s - BIAS_LAG[1])
             run(add_bias, 2, s - BIAS_LAG[2])
-            means(s - 1)
-            run(transpose_combined, s - 5)
-            run(sum_squares, 1, s - 3)
-            run(sum_squares, 2, s - 8)
-            run(centre, s - 4)
-            run(quantise_z, s - 1)
-            run(quantise_combined, s - 6)
-            run(project, s - 4)
-            run(normalise, s - 9)
-            run(gelu_by_feature, s - 10)
+            run(sum_squares, 1, s - 4)
+            run(sum_squares, 2, s - 9)
+            run(centre, s - 5)
+            run(normalise, s - 10)
+            run(project, s - 5)
+            run(transpose_combined, s - 6)
+            run(gelu_by_feature, s - 11)
             deviations(s - 1)
             run(store_by_token, s - LAST_LAG)
             run(transpose_z, s)
+            means(s)

@@ -171,7 +171,10 @@ def tile_synapsemodel_pa_t_kernel(
             layers = layers_of_step(t)
             if layers is not None:
                 neg_mean = lasting.tile([P, 2, PAIR], F32, name="neg_mean")
-                nc.scalar.mul(out=neg_mean[:, layers], in_=held["row_sum", t][:, layers], mul=-1.0 / H)
+                nc.gpsimd.tensor_scalar(
+                    out=neg_mean[:, layers], in0=held["row_sum", t][:, layers],
+                    scalar1=-1.0 / H, scalar2=0.0, op0=ALU.mult, op1=ALU.add,
+                )
                 held["neg_mean", t] = neg_mean
                 held["square_sum", t] = lasting.tile([P, 2, PAIR], F32, name="square_sum")
 
@@ -192,9 +195,9 @@ def tile_synapsemodel_pa_t_kernel(
             layers = layers_of_step(t)
             if layers is not None:
                 variance_eps = lasting.tile([P, 2, PAIR], F32, name="variance_eps")
-                nc.scalar.activation(
-                    out=variance_eps[:, layers], in_=held["square_sum", t][:, layers],
-                    func=ACT.Copy, bias=LN_EPS, scale=1.0 / H,
+                nc.gpsimd.tensor_scalar(
+                    out=variance_eps[:, layers], in0=held["square_sum", t][:, layers],
+                    scalar1=1.0 / H, scalar2=LN_EPS, op0=ALU.mult, op1=ALU.add,
                 )
                 rstd = lasting.tile([P, 2, PAIR], F32, name="rstd")
                 nc.gpsimd.tensor_tensor(
@@ -261,7 +264,7 @@ def tile_synapsemodel_pa_t_kernel(
             t = u + BIAS_LAG[2]
             normed = brief.tile([P, PAIR, H], F32, name="normed")
             for i in range(PAIR):
-                nc.vector.tensor_scalar(
+                nc.gpsimd.tensor_scalar(
                     out=normed[:, i, :], in0=held["x", 2, u][:, i, :],
                     scalar1=held["neg_mean", t][:, 1, i : i + 1], scalar2=held["rstd", t][:, 1, i : i + 1],
                     op0=ALU.add, op1=ALU.mult,

@@ -24,6 +24,9 @@ PAIR = 2
 UNITS = N_TOKENS // (P * PAIR)
 LOAD_AHEAD = 3
 LAST_LAG = 12
+FIRST_VECTOR_STEP = 3
+ROW_VECTORS = ("bz", "gz", "bz_ln", "b1")
+Z_BANKS = 3
 BIAS_LAG = {1: 3, 2: 8}
 
 FLOPS = 2 * N_TOKENS * D * H + 2 * N_TOKENS * (2 * H) * H
@@ -45,12 +48,6 @@ def load_weight(nc, const, words, scales, passes, name):
     return codes, plane
 
 
-def load_row(nc, const, vector, name):
-    row = const.tile([P, H], BF16, name=name)
-    nc.scalar.dma_start(out=row[:], in_=vector.partition_broadcast(P))
-    return row
-
-
 def transpose_words(nc, bank, token_words, identity):
     for u in range(2):
         nc.tensor.transpose(bank[:, u, :], token_words[:, u:WORDS:2], identity[:])
@@ -68,51 +65,73 @@ def tile_synapsemodel_pa_t_kernel(
         const = stack.enter_context(tc.tile_pool(name="const", bufs=1))
         brief = stack.enter_context(tc.tile_pool(name="brief", bufs=3))
         lasting = stack.enter_context(tc.tile_pool(name="lasting", bufs=5))
-        longest = stack.enter_context(tc.tile_pool(name="longest", bufs=12))
         psum = stack.enter_context(tc.psum_pool(name="psum", bufs=1))
 
         held = {}
 
-        def load(u):
+        def load_z(u):
             z_rows = lasting.tile([P, PAIR, D], BF16, name="z_rows")
             nc.sync.dma_start(out=z_rows[:], in_=z_units[u])
-            combined = longest.tile([P, PAIR, 2 * H], BF16, name="combined")
-            nc.sync.dma_start(out=combined[:, :, H : 2 * H], in_=attention_units[u])
             held["z_rows", u] = z_rows
+
+        def load_attention(u):
+            combined = lasting.tile([P, PAIR, 2 * H], BF16, name="combined")
+            nc.sync.dma_start(out=combined[:, :, H : 2 * H], in_=attention_units[u])
             held["combined", u] = combined
 
         stack.enter_context(tc.manual_schedule())
 
-        load(0)
+        load_z(0)
+        load_z(1)
+        wz_codes, wz_scales = load_weight(nc, const, Wz_words, Wz_scales, Z_PASSES, "wz")
+        load_z(2)
+        w1_codes, w1_scales = load_weight(nc, const, w1_deq_words, w1_deq_scales, 1, "w1")
+
         identity = const.tile([P, P], F32)
         make_identity(nc, identity[:])
-        vector_rows = const.tile([P, P], BF16)
-        nc.vector.memset(vector_rows[:], 0.0)
-        nc.scalar.dma_start(out=vector_rows[0:HALVES, :], in_=g1.rearrange("(h f) -> h f", h=HALVES))
-        nc.scalar.dma_start(out=vector_rows[HALVES : 2 * HALVES, :], in_=b1_ln.rearrange("(h f) -> h f", h=HALVES))
-        wz_codes, wz_scales = load_weight(nc, const, Wz_words, Wz_scales, Z_PASSES, "wz")
-        w1_codes, w1_scales = load_weight(nc, const, w1_deq_words, w1_deq_scales, 1, "w1")
-        bias_row = {1: load_row(nc, const, bz, "bz_row"), 2: load_row(nc, const, b1, "b1_row")}
-        gz_row = load_row(nc, const, gz, "gz_row")
-        bz_ln_row = load_row(nc, const, bz_ln, "bz_ln_row")
         minus_half = const.tile([P, 2, PAIR], F32)
         nc.vector.memset(minus_half[:], -0.5)
-        vector_rows_f32 = const.tile([P, P], F32)
-        nc.vector.tensor_copy(out=vector_rows_f32[:], in_=vector_rows[:])
-        column_bank = psum.tile([P, P], F32)
-        nc.tensor.transpose(column_bank[:], vector_rows_f32[:], identity[:])
-        vector_columns = const.tile([P, 2 * HALVES], F32)
-        nc.vector.tensor_copy(out=vector_columns[:], in_=column_bank[:, 0 : 2 * HALVES])
-        g1_columns = vector_columns[:, 0:HALVES]
-        b1_ln_columns = vector_columns[:, HALVES : 2 * HALVES]
-        for u in range(1, LOAD_AHEAD):
-            load(u)
+
+        ones = const.tile([P, P], BF16)
+        nc.vector.memset(ones[:], 1.0)
+        row_source = const.tile([P, len(ROW_VECTORS), H], BF16)
+        nc.vector.memset(row_source[:], 0.0)
+        given = {"bz": bz, "gz": gz, "bz_ln": bz_ln, "b1": b1}
+        for j, name in enumerate(ROW_VECTORS):
+            nc.scalar.dma_start(out=row_source[0:1, j, :], in_=given[name].unsqueeze(0))
+        column_source = const.tile([P, P], BF16)
+        nc.vector.memset(column_source[:], 0.0)
+        nc.scalar.dma_start(out=column_source[0:HALVES, :], in_=g1.rearrange("(h f) -> h f", h=HALVES))
+        nc.scalar.dma_start(out=column_source[HALVES : 2 * HALVES, :], in_=b1_ln.rearrange("(h f) -> h f", h=HALVES))
+        rows = const.tile([P, len(ROW_VECTORS), H], F32)
+        columns = const.tile([P, 2 * HALVES], F32)
+        row_of = {name: rows[:, j, :] for j, name in enumerate(ROW_VECTORS)}
+        bias_row = {1: row_of["bz"], 2: row_of["b1"]}
+        g1_columns = columns[:, 0:HALVES]
+        b1_ln_columns = columns[:, HALVES : 2 * HALVES]
+
+        def spread_vectors():
+            for first in range(0, len(ROW_VECTORS), PAIR):
+                row_bank = psum.tile([P, PAIR, H], F32, name="y1_bank")
+                nc.tensor.matmul(
+                    out=row_bank[:].rearrange("p j h -> p (j h)"),
+                    lhsT=ones[:],
+                    rhs=row_source[:, first : first + PAIR, :].rearrange("p j h -> p (j h)"),
+                    start=True,
+                    stop=True,
+                )
+                nc.scalar.copy(out=rows[:, first : first + PAIR, :], in_=row_bank[:])
+            column_source_f32 = const.tile([P, P], F32)
+            nc.vector.tensor_copy(out=column_source_f32[:], in_=column_source[:])
+            column_bank = psum.tile([P, PAIR, H], F32, name="token_bank")
+            nc.tensor.transpose(column_bank[:, 0, 0:P], column_source_f32[:], identity[:])
+            nc.vector.tensor_copy(out=columns[:], in_=column_bank[:, 0, 0 : 2 * HALVES])
 
         def transpose_z(u):
             z_words = held["z_rows", u][:].bitcast(F32)
             z_grouped = lasting.tile([P, PAIR, Z_PASSES, P, PACK], BF16, name="z_grouped", align_bytes=64)
             for i in range(PAIR):
-                z_bank = psum.tile([P, Z_PASSES, 2, P], F32, name="z_bank", bufs=PAIR)
+                z_bank = psum.tile([P, Z_PASSES, 2, P], F32, name="z_bank", bufs=Z_BANKS)
                 for g in range(Z_PASSES):
                     transpose_words(nc, z_bank[:, g], z_words[:, i, WORDS * g : WORDS * (g + 1)], identity)
                 nc.scalar.copy(out=z_grouped[:, i].bitcast(F32), in_=z_bank[:].rearrange("p g u r -> p g r u"))
@@ -160,7 +179,7 @@ def tile_synapsemodel_pa_t_kernel(
                     out=x[:, i, :],
                     in0=y_bank[:, i, :],
                     scalar=1.0,
-                    in1=bias_row[layer][:],
+                    in1=bias_row[layer],
                     op0=ALU.mult,
                     op1=ALU.add,
                     accum_out=held["row_sum", t][:, layer - 1, i : i + 1],
@@ -171,10 +190,7 @@ def tile_synapsemodel_pa_t_kernel(
             layers = layers_of_step(t)
             if layers is not None:
                 neg_mean = lasting.tile([P, 2, PAIR], F32, name="neg_mean")
-                nc.gpsimd.tensor_scalar(
-                    out=neg_mean[:, layers], in0=held["row_sum", t][:, layers],
-                    scalar1=-1.0 / H, scalar2=0.0, op0=ALU.mult, op1=ALU.add,
-                )
+                nc.scalar.mul(out=neg_mean[:, layers], in_=held["row_sum", t][:, layers], mul=-1.0 / H)
                 held["neg_mean", t] = neg_mean
                 held["square_sum", t] = lasting.tile([P, 2, PAIR], F32, name="square_sum")
 
@@ -195,9 +211,9 @@ def tile_synapsemodel_pa_t_kernel(
             layers = layers_of_step(t)
             if layers is not None:
                 variance_eps = lasting.tile([P, 2, PAIR], F32, name="variance_eps")
-                nc.gpsimd.tensor_scalar(
-                    out=variance_eps[:, layers], in0=held["square_sum", t][:, layers],
-                    scalar1=1.0 / H, scalar2=LN_EPS, op0=ALU.mult, op1=ALU.add,
+                nc.scalar.activation(
+                    out=variance_eps[:, layers], in_=held["square_sum", t][:, layers],
+                    func=ACT.Copy, bias=LN_EPS, scale=1.0 / H,
                 )
                 rstd = lasting.tile([P, 2, PAIR], F32, name="rstd")
                 nc.gpsimd.tensor_tensor(
@@ -211,7 +227,7 @@ def tile_synapsemodel_pa_t_kernel(
             for i in range(PAIR):
                 nc.vector.scalar_tensor_tensor(
                     out=centred[:, i, :], in0=held["x", 1, u][:, i, :],
-                    scalar=neg_mean[:, 0, i : i + 1], in1=gz_row[:],
+                    scalar=neg_mean[:, 0, i : i + 1], in1=row_of["gz"],
                     op0=ALU.add, op1=ALU.mult,
                 )
             held["centred", u] = centred
@@ -221,7 +237,7 @@ def tile_synapsemodel_pa_t_kernel(
             for i in range(PAIR):
                 nc.vector.scalar_tensor_tensor(
                     out=held["combined", u][:, i, 0:H], in0=held["centred", u][:, i, :],
-                    scalar=rstd[:, 0, i : i + 1], in1=bz_ln_row[:],
+                    scalar=rstd[:, 0, i : i + 1], in1=row_of["bz_ln"],
                     op0=ALU.mult, op1=ALU.add,
                 )
 
@@ -264,7 +280,7 @@ def tile_synapsemodel_pa_t_kernel(
             t = u + BIAS_LAG[2]
             normed = brief.tile([P, PAIR, H], F32, name="normed")
             for i in range(PAIR):
-                nc.gpsimd.tensor_scalar(
+                nc.vector.tensor_scalar(
                     out=normed[:, i, :], in0=held["x", 2, u][:, i, :],
                     scalar1=held["neg_mean", t][:, 1, i : i + 1], scalar2=held["rstd", t][:, 1, i : i + 1],
                     op0=ALU.add, op1=ALU.mult,
@@ -303,8 +319,9 @@ def tile_synapsemodel_pa_t_kernel(
             if 0 <= unit[-1] < UNITS:
                 stage(*unit)
 
-        for s in range(UNITS + LAST_LAG + 1):
-            run(load, s + LOAD_AHEAD)
+        def step(s):
+            run(load_z, s + LOAD_AHEAD)
+            run(load_attention, s - 3)
             run(quantise_z, s - 2)
             run(quantise_combined, s - 7)
             run(multiply_z, s - 3)
@@ -322,3 +339,9 @@ def tile_synapsemodel_pa_t_kernel(
             run(store_by_token, s - LAST_LAG)
             run(transpose_z, s)
             means(s)
+
+        for s in range(FIRST_VECTOR_STEP - 1):
+            step(s)
+        spread_vectors()
+        for s in range(FIRST_VECTOR_STEP - 1, UNITS + LAST_LAG + 1):
+            step(s)

@@ -25,8 +25,9 @@ UNITS = N_TOKENS // (P * PAIR)
 LOAD_AHEAD = 3
 LAST_LAG = 12
 FIRST_VECTOR_STEP = 3
-ROW_VECTORS = ("bz", "gz", "bz_ln", "b1")
-Z_BANKS = 3
+ROW_VECTORS = ("bz", "b1", "gz", "bz_ln")
+SBUF_ROWS = 2
+Z_BANKS = 2
 BIAS_LAG = {1: 3, 2: 8}
 
 FLOPS = 2 * N_TOKENS * D * H + 2 * N_TOKENS * (2 * H) * H
@@ -103,24 +104,25 @@ def tile_synapsemodel_pa_t_kernel(
         nc.vector.memset(column_source[:], 0.0)
         nc.scalar.dma_start(out=column_source[0:HALVES, :], in_=g1.rearrange("(h f) -> h f", h=HALVES))
         nc.scalar.dma_start(out=column_source[HALVES : 2 * HALVES, :], in_=b1_ln.rearrange("(h f) -> h f", h=HALVES))
-        rows = const.tile([P, len(ROW_VECTORS), H], F32)
+        rows = const.tile([P, SBUF_ROWS, H], F32)
+        ln1_rows = psum.tile([P, PAIR, H], F32, name="ln1_rows")
         columns = const.tile([P, 2 * HALVES], F32)
-        row_of = {name: rows[:, j, :] for j, name in enumerate(ROW_VECTORS)}
+        row_of = {"bz": rows[:, 0, :], "b1": rows[:, 1, :], "gz": ln1_rows[:, 0, :], "bz_ln": ln1_rows[:, 1, :]}
         bias_row = {1: row_of["bz"], 2: row_of["b1"]}
         g1_columns = columns[:, 0:HALVES]
         b1_ln_columns = columns[:, HALVES : 2 * HALVES]
 
         def spread_vectors():
-            for first in range(0, len(ROW_VECTORS), PAIR):
-                row_bank = psum.tile([P, PAIR, H], F32, name="y1_bank")
+            row_bank = psum.tile([P, PAIR, H], F32, name="y1_bank")
+            for first, bank in ((0, row_bank), (SBUF_ROWS, ln1_rows)):
                 nc.tensor.matmul(
-                    out=row_bank[:].rearrange("p j h -> p (j h)"),
+                    out=bank[:].rearrange("p j h -> p (j h)"),
                     lhsT=ones[:],
                     rhs=row_source[:, first : first + PAIR, :].rearrange("p j h -> p (j h)"),
                     start=True,
                     stop=True,
                 )
-                nc.scalar.copy(out=rows[:, first : first + PAIR, :], in_=row_bank[:])
+            nc.scalar.copy(out=rows[:], in_=row_bank[:])
             column_source_f32 = const.tile([P, P], F32)
             nc.vector.tensor_copy(out=column_source_f32[:], in_=column_source[:])
             column_bank = psum.tile([P, PAIR, H], F32, name="token_bank")

@@ -192,7 +192,10 @@ def tile_synapsemodel_pa_t_kernel(
             layers = layers_of_step(t)
             if layers is not None:
                 neg_mean = lasting.tile([P, 2, PAIR], F32, name="neg_mean")
-                nc.scalar.mul(out=neg_mean[:, layers], in_=held["row_sum", t][:, layers], mul=-1.0 / H)
+                nc.gpsimd.tensor_scalar(
+                    out=neg_mean[:, layers], in0=held["row_sum", t][:, layers],
+                    scalar1=-1.0 / H, scalar2=0.0, op0=ALU.mult, op1=ALU.add,
+                )
                 held["neg_mean", t] = neg_mean
                 held["square_sum", t] = lasting.tile([P, 2, PAIR], F32, name="square_sum")
 
@@ -204,8 +207,8 @@ def tile_synapsemodel_pa_t_kernel(
                     out=squares[:],
                     in_=held["x", layer, u][:, i, :],
                     func=ACT.Square,
-                    bias=held["neg_mean", t][:, layer - 1, i : i + 1],
-                    scale=1.0,
+                    bias=held["row_sum", t][:, layer - 1, i : i + 1],
+                    scale=-1.0 * H,
                     accum_out=held["square_sum", t][:, layer - 1, i : i + 1],
                 )
 
@@ -215,7 +218,7 @@ def tile_synapsemodel_pa_t_kernel(
                 variance_eps = lasting.tile([P, 2, PAIR], F32, name="variance_eps")
                 nc.scalar.activation(
                     out=variance_eps[:, layers], in_=held["square_sum", t][:, layers],
-                    func=ACT.Copy, bias=LN_EPS, scale=1.0 / H,
+                    func=ACT.Copy, bias=LN_EPS, scale=1.0 / (H * H * H),
                 )
                 rstd = lasting.tile([P, 2, PAIR], F32, name="rstd")
                 nc.gpsimd.tensor_tensor(

@@ -314,10 +314,7 @@ def tile_synapsemodel_pa_t_kernel(
                 for h in range(HALVES):
                     nc.tensor.transpose(token_bank[:, i, P * h : P * (h + 1)], held["activated", u][:, h, i, :], identity[:])
             result = brief.tile([P, PAIR, H], F32, name="result")
-            if u % 2 == 0:
-                nc.scalar.copy(out=result[:], in_=token_bank[:])
-            else:
-                nc.vector.tensor_copy(out=result[:], in_=token_bank[:])
+            nc.scalar.copy(out=result[:], in_=token_bank[:])
             nc.sync.dma_start(out=out_units[u], in_=result[:])
 
         def run(stage, *unit):

@@ -216,9 +216,9 @@ def tile_synapsemodel_pa_t_kernel(
             layers = layers_of_step(t)
             if layers is not None:
                 variance_eps = lasting.tile([P, 2, PAIR], F32, name="variance_eps")
-                nc.scalar.activation(
-                    out=variance_eps[:, layers], in_=held["square_sum", t][:, layers],
-                    func=ACT.Copy, bias=LN_EPS, scale=1.0 / (H * H * H),
+                nc.gpsimd.tensor_scalar(
+                    out=variance_eps[:, layers], in0=held["square_sum", t][:, layers],
+                    scalar1=1.0 / (H * H * H), scalar2=LN_EPS, op0=ALU.mult, op1=ALU.add,
                 )
                 rstd = lasting.tile([P, 2, PAIR], F32, name="rstd")
                 nc.gpsimd.tensor_tensor(
@@ -314,7 +314,10 @@ def tile_synapsemodel_pa_t_kernel(
                 for h in range(HALVES):
                     nc.tensor.transpose(token_bank[:, i, P * h : P * (h + 1)], held["activated", u][:, h, i, :], identity[:])
             result = brief.tile([P, PAIR, H], F32, name="result")
-            nc.scalar.copy(out=result[:], in_=token_bank[:])
+            if u % 8 == 7:
+                nc.vector.tensor_copy(out=result[:], in_=token_bank[:])
+            else:
+                nc.scalar.copy(out=result[:], in_=token_bank[:])
             nc.sync.dma_start(out=out_units[u], in_=result[:])
 
         def run(stage, *unit):
@@ -332,12 +335,12 @@ def tile_synapsemodel_pa_t_kernel(
             run(add_bias, 2, s - BIAS_LAG[2])
             run(sum_squares, 1, s - 4)
             run(sum_squares, 2, s - 9)
+            deviations(s - 1)
             run(centre, s - 5)
             run(normalise, s - 10)
             run(project, s - 5)
             run(transpose_combined, s - 6)
             run(gelu_by_feature, s - 11)
-            deviations(s - 1)
             run(store_by_token, s - LAST_LAG)
             run(transpose_z, s)
             means(s)

@@ -28,6 +28,7 @@ FIRST_VECTOR_STEP = 3
 ROW_VECTORS = ("bz", "b1", "gz", "bz_ln")
 SBUF_ROWS = 2
 Z_BANKS = 2
+SQUARE_BUFS = 16
 BIAS_LAG = {1: 3, 2: 8}
 
 FLOPS = 2 * N_TOKENS * D * H + 2 * N_TOKENS * (2 * H) * H
@@ -82,6 +83,11 @@ def tile_synapsemodel_pa_t_kernel(
 
         stack.enter_context(tc.manual_schedule())
 
+        minus_half = const.tile([P, 2, PAIR], F32)
+        nc.vector.memset(minus_half[:], -0.5)
+        table_loader = const.tile([P, 1], F32)
+        nc.scalar.activation(out=table_loader[:], in_=minus_half[:, 0, 0:1], func=ACT.Gelu)
+
         load_z(0)
         load_z(1)
         wz_codes, wz_scales = load_weight(nc, const, Wz_words, Wz_scales, Z_PASSES, "wz")
@@ -90,8 +96,6 @@ def tile_synapsemodel_pa_t_kernel(
 
         identity = const.tile([P, P], F32)
         make_identity(nc, identity[:])
-        minus_half = const.tile([P, 2, PAIR], F32)
-        nc.vector.memset(minus_half[:], -0.5)
 
         ones = const.tile([P, P], BF16)
         nc.vector.memset(ones[:], 1.0)
@@ -202,7 +206,7 @@ def tile_synapsemodel_pa_t_kernel(
         def sum_squares(layer, u):
             t = u + BIAS_LAG[layer]
             for i in range(PAIR):
-                squares = lasting.tile([P, H], BF16, name="squares")
+                squares = lasting.tile([P, H], BF16, name="squares", bufs=SQUARE_BUFS)
                 nc.scalar.activation(
                     out=squares[:],
                     in_=held["x", layer, u][:, i, :],
@@ -313,7 +317,7 @@ def tile_synapsemodel_pa_t_kernel(
             for i in range(PAIR):
                 for h in range(HALVES):
                     nc.tensor.transpose(token_bank[:, i, P * h : P * (h + 1)], held["activated", u][:, h, i, :], identity[:])
-            result = brief.tile([P, PAIR, H], F32, name="result")
+            result = brief.tile([P, PAIR, H], F32, name="result", bufs=UNITS)
             if u % 8 == 7:
                 nc.vector.tensor_copy(out=result[:], in_=token_bank[:])
             else:

@@ -24,7 +24,8 @@ PAIR = 2
 UNITS = N_TOKENS // (P * PAIR)
 LOAD_AHEAD = 3
 LAST_LAG = 12
-FIRST_VECTOR_STEP = 3
+FIRST_ROW_STEP = 3
+FIRST_COLUMN_STEP = 4
 ROW_VECTORS = ("bz", "b1", "gz", "bz_ln")
 SBUF_ROWS = 2
 Z_BANKS = 2
@@ -85,29 +86,30 @@ def tile_synapsemodel_pa_t_kernel(
 
         minus_half = const.tile([P, 2, PAIR], F32)
         nc.vector.memset(minus_half[:], -0.5)
+        row_source = const.tile([P, len(ROW_VECTORS), H], BF16)
+        nc.vector.memset(row_source[:], 0.0)
+        column_source = const.tile([P, P], BF16)
+        nc.vector.memset(column_source[:], 0.0)
+        ones = const.tile([P, P], BF16)
+        nc.vector.memset(ones[:], 1.0)
+
         table_loader = const.tile([P, 1], F32)
         nc.scalar.activation(out=table_loader[:], in_=minus_half[:, 0, 0:1], func=ACT.Gelu)
-
-        load_z(0)
-        load_z(1)
-        wz_codes, wz_scales = load_weight(nc, const, Wz_words, Wz_scales, Z_PASSES, "wz")
-        load_z(2)
-        w1_codes, w1_scales = load_weight(nc, const, w1_deq_words, w1_deq_scales, 1, "w1")
 
         identity = const.tile([P, P], F32)
         make_identity(nc, identity[:])
 
-        ones = const.tile([P, P], BF16)
-        nc.vector.memset(ones[:], 1.0)
-        row_source = const.tile([P, len(ROW_VECTORS), H], BF16)
-        nc.vector.memset(row_source[:], 0.0)
+        load_z(0)
         given = {"bz": bz, "gz": gz, "bz_ln": bz_ln, "b1": b1}
         for j, name in enumerate(ROW_VECTORS):
-            nc.scalar.dma_start(out=row_source[0:1, j, :], in_=given[name].unsqueeze(0))
-        column_source = const.tile([P, P], BF16)
-        nc.vector.memset(column_source[:], 0.0)
-        nc.scalar.dma_start(out=column_source[0:HALVES, :], in_=g1.rearrange("(h f) -> h f", h=HALVES))
-        nc.scalar.dma_start(out=column_source[HALVES : 2 * HALVES, :], in_=b1_ln.rearrange("(h f) -> h f", h=HALVES))
+            nc.sync.dma_start(out=row_source[0:1, j, :], in_=given[name].unsqueeze(0))
+        load_z(1)
+        wz_codes, wz_scales = load_weight(nc, const, Wz_words, Wz_scales, Z_PASSES, "wz")
+        load_z(2)
+        nc.sync.dma_start(out=column_source[0:HALVES, :], in_=g1.rearrange("(h f) -> h f", h=HALVES))
+        nc.sync.dma_start(out=column_source[HALVES : 2 * HALVES, :], in_=b1_ln.rearrange("(h f) -> h f", h=HALVES))
+        w1_codes, w1_scales = load_weight(nc, const, w1_deq_words, w1_deq_scales, 1, "w1")
+
         rows = const.tile([P, SBUF_ROWS, H], F32)
         ln1_rows = psum.tile([P, PAIR, H], F32, name="ln1_rows")
         columns = const.tile([P, 2 * HALVES], F32)
@@ -116,7 +118,7 @@ def tile_synapsemodel_pa_t_kernel(
         g1_columns = columns[:, 0:HALVES]
         b1_ln_columns = columns[:, HALVES : 2 * HALVES]
 
-        def spread_vectors():
+        def spread_rows():
             row_bank = psum.tile([P, PAIR, H], F32, name="y1_bank")
             for first, bank in ((0, row_bank), (SBUF_ROWS, ln1_rows)):
                 nc.tensor.matmul(
@@ -127,11 +129,15 @@ def tile_synapsemodel_pa_t_kernel(
                     stop=True,
                 )
             nc.scalar.copy(out=rows[:], in_=row_bank[:])
+        def spread_columns():
             column_source_f32 = const.tile([P, P], F32)
             nc.vector.tensor_copy(out=column_source_f32[:], in_=column_source[:])
             column_bank = psum.tile([P, PAIR, H], F32, name="token_bank")
             nc.tensor.transpose(column_bank[:, 0, 0:P], column_source_f32[:], identity[:])
-            nc.vector.tensor_copy(out=columns[:], in_=column_bank[:, 0, 0 : 2 * HALVES])
+            held["column_bank"] = column_bank
+
+        def copy_columns():
+            nc.vector.tensor_copy(out=columns[:], in_=held["column_bank"][:, 0, 0 : 2 * HALVES])
 
         def transpose_z(u):
             z_words = held["z_rows", u][:].bitcast(F32)
@@ -174,6 +180,9 @@ def tile_synapsemodel_pa_t_kernel(
             live = [layer - 1 for layer in (1, 2) if 0 <= t - BIAS_LAG[layer] < UNITS]
             return slice(live[0], live[-1] + 1) if live else None
 
+        def statistics_engine(layers):
+            return nc.gpsimd if layers.start == 0 else nc.vector
+
         def add_bias(layer, u):
             t = u + BIAS_LAG[layer]
             if ("row_sum", t) not in held:
@@ -196,7 +205,7 @@ def tile_synapsemodel_pa_t_kernel(
             layers = layers_of_step(t)
             if layers is not None:
                 neg_mean = lasting.tile([P, 2, PAIR], F32, name="neg_mean")
-                nc.gpsimd.tensor_scalar(
+                statistics_engine(layers).tensor_scalar(
                     out=neg_mean[:, layers], in0=held["row_sum", t][:, layers],
                     scalar1=-1.0 / H, scalar2=0.0, op0=ALU.mult, op1=ALU.add,
                 )
@@ -220,7 +229,7 @@ def tile_synapsemodel_pa_t_kernel(
             layers = layers_of_step(t)
             if layers is not None:
                 variance_eps = lasting.tile([P, 2, PAIR], F32, name="variance_eps")
-                nc.gpsimd.tensor_scalar(
+                statistics_engine(layers).tensor_scalar(
                     out=variance_eps[:, layers], in0=held["square_sum", t][:, layers],
                     scalar1=1.0 / (H * H * H), scalar2=LN_EPS, op0=ALU.mult, op1=ALU.add,
                 )
@@ -337,10 +346,10 @@ def tile_synapsemodel_pa_t_kernel(
             run(multiply_combined, s - 8)
             run(add_bias, 1, s - BIAS_LAG[1])
             run(add_bias, 2, s - BIAS_LAG[2])
+            run(centre, s - 4)
             run(sum_squares, 1, s - 4)
             run(sum_squares, 2, s - 9)
             deviations(s - 1)
-            run(centre, s - 5)
             run(normalise, s - 10)
             run(project, s - 5)
             run(transpose_combined, s - 6)
@@ -349,8 +358,11 @@ def tile_synapsemodel_pa_t_kernel(
             run(transpose_z, s)
             means(s)
 
-        for s in range(FIRST_VECTOR_STEP - 1):
-            step(s)
-        spread_vectors()
-        for s in range(FIRST_VECTOR_STEP - 1, UNITS + LAST_LAG + 1):
+        for s in range(UNITS + LAST_LAG + 1):
+            if s == FIRST_ROW_STEP - 1:
+                spread_rows()
+            if s == FIRST_COLUMN_STEP:
+                spread_columns()
+            if s == FIRST_COLUMN_STEP + 2:
+                copy_columns()
             step(s)

@@ -23,13 +23,15 @@ LN_EPS = 1e-5
 PAIR = 2
 UNITS = N_TOKENS // (P * PAIR)
 LOAD_AHEAD = 3
-LAST_LAG = 12
+LAST_LAG = 13
 FIRST_ROW_STEP = 3
 FIRST_COLUMN_STEP = 4
 ROW_VECTORS = ("bz", "b1", "gz", "bz_ln")
 SBUF_ROWS = 2
 Z_BANKS = 2
 SQUARE_BUFS = 16
+PROJECT_LAG = 5
+NORMALISE_LAG = 11
 BIAS_LAG = {1: 3, 2: 8}
 
 FLOPS = 2 * N_TOKENS * D * H + 2 * N_TOKENS * (2 * H) * H
@@ -296,9 +298,10 @@ def tile_synapsemodel_pa_t_kernel(
 
         def normalise(u):
             t = u + BIAS_LAG[2]
+            engine = nc.gpsimd if u + NORMALISE_LAG < UNITS + PROJECT_LAG else nc.vector
             normed = brief.tile([P, PAIR, H], F32, name="normed")
             for i in range(PAIR):
-                nc.vector.tensor_scalar(
+                engine.tensor_scalar(
                     out=normed[:, i, :], in0=held["x", 2, u][:, i, :],
                     scalar1=held["neg_mean", t][:, 1, i : i + 1], scalar2=held["rstd", t][:, 1, i : i + 1],
                     op0=ALU.add, op1=ALU.mult,
@@ -327,7 +330,7 @@ def tile_synapsemodel_pa_t_kernel(
                 for h in range(HALVES):
                     nc.tensor.transpose(token_bank[:, i, P * h : P * (h + 1)], held["activated", u][:, h, i, :], identity[:])
             result = brief.tile([P, PAIR, H], F32, name="result", bufs=UNITS)
-            if u % 8 == 7:
+            if u % 5 in (1, 3):
                 nc.vector.tensor_copy(out=result[:], in_=token_bank[:])
             else:
                 nc.scalar.copy(out=result[:], in_=token_bank[:])
@@ -340,6 +343,7 @@ def tile_synapsemodel_pa_t_kernel(
         def step(s):
             run(load_z, s + LOAD_AHEAD)
             run(load_attention, s - 3)
+            run(normalise, s - NORMALISE_LAG)
             run(quantise_z, s - 2)
             run(quantise_combined, s - 7)
             run(multiply_z, s - 3)
@@ -350,10 +354,9 @@ def tile_synapsemodel_pa_t_kernel(
             run(sum_squares, 1, s - 4)
             run(sum_squares, 2, s - 9)
             deviations(s - 1)
-            run(normalise, s - 10)
-            run(project, s - 5)
+            run(project, s - PROJECT_LAG)
             run(transpose_combined, s - 6)
-            run(gelu_by_feature, s - 11)
+            run(gelu_by_feature, s - 12)
             run(store_by_token, s - LAST_LAG)
             run(transpose_z, s)
             means(s)

@@ -227,6 +227,9 @@ def tile_synapsemodel_pa_t_kernel(
                     accum_out=held["square_sum", t][:, layer - 1, i : i + 1],
                 )
 
+        def normalised_on_gpsimd(u):
+            return 0 <= u < UNITS and u + NORMALISE_LAG < UNITS + PROJECT_LAG
+
         def deviations(t):
             layers = layers_of_step(t)
             if layers is not None:
@@ -240,6 +243,10 @@ def tile_synapsemodel_pa_t_kernel(
                     out=rstd[:, layers], in0=variance_eps[:, layers], in1=minus_half[:, layers], op=ALU.pow
                 )
                 held["rstd", t] = rstd
+                if normalised_on_gpsimd(t - BIAS_LAG[2]):
+                    shift = lasting.tile([P, PAIR], F32, name="shift")
+                    nc.gpsimd.tensor_tensor(out=shift[:], in0=held["neg_mean", t][:, 1], in1=rstd[:, 1], op=ALU.mult)
+                    held["shift", t] = shift
 
         def centre(u):
             neg_mean = held["neg_mean", u + BIAS_LAG[1]]
@@ -298,14 +305,20 @@ def tile_synapsemodel_pa_t_kernel(
 
         def normalise(u):
             t = u + BIAS_LAG[2]
-            engine = nc.gpsimd if u + NORMALISE_LAG < UNITS + PROJECT_LAG else nc.vector
             normed = brief.tile([P, PAIR, H], F32, name="normed")
             for i in range(PAIR):
-                engine.tensor_scalar(
-                    out=normed[:, i, :], in0=held["x", 2, u][:, i, :],
-                    scalar1=held["neg_mean", t][:, 1, i : i + 1], scalar2=held["rstd", t][:, 1, i : i + 1],
-                    op0=ALU.add, op1=ALU.mult,
-                )
+                x = held["x", 2, u][:, i, :]
+                rstd = held["rstd", t][:, 1, i : i + 1]
+                if normalised_on_gpsimd(u):
+                    nc.gpsimd.tensor_scalar(
+                        out=normed[:, i, :], in0=x, scalar1=rstd, scalar2=held["shift", t][:, i : i + 1],
+                        op0=ALU.mult, op1=ALU.add,
+                    )
+                else:
+                    nc.vector.tensor_scalar(
+                        out=normed[:, i, :], in0=x, scalar1=held["neg_mean", t][:, 1, i : i + 1], scalar2=rstd,
+                        op0=ALU.add, op1=ALU.mult,
+                    )
             held["normed", u] = normed
 
         def gelu_by_feature(u):

from contextlib import ExitStack

import concourse.mybir as mybir
from concourse.masks import make_identity

F32 = mybir.dt.float32
BF16 = mybir.dt.bfloat16
I32 = mybir.dt.int32
U32 = mybir.dt.uint32
U8 = mybir.dt.uint8
FP8X4 = mybir.dt.float8_e4m3fn_x4
ALU = mybir.AluOpType
ACT = mybir.ActivationFunctionType

P = 128
PACK = 4
K_PASS = P * PACK
WORDS = K_PASS // 2
N_TOKENS, D, H = 8192, 1024, 256
Z_PASSES = D // K_PASS
HALVES = H // P
LN_EPS = 1e-5
PAIR = 2
UNITS = N_TOKENS // (P * PAIR)
LOAD_AHEAD = 3
LAST_LAG = 13
FIRST_ROW_STEP = 3
FIRST_COLUMN_STEP = 4
ROW_VECTORS = ("bz", "b1", "gz", "bz_ln")
SBUF_ROWS = 2
Z_BANKS = 2
SQUARE_BUFS = 16
PROJECT_LAG = 5
NORMALISE_LAG = 11
BIAS_LAG = {1: 3, 2: 8}

FLOPS = 2 * N_TOKENS * D * H + 2 * N_TOKENS * (2 * H) * H


def load_weight(nc, const, words, scales, passes, name):
    codes = const.tile([P, passes, H], U32, name=name + "_codes", align_bytes=64)
    nc.sync.dma_start(
        out=codes[:].bitcast(I32),
        in_=words.rearrange("g p n t -> p g (n t)").bitcast(I32),
    )
    plane = const.tile([P, passes, H], U8, name=name + "_scales", align_bytes=64)
    nc.vector.memset(plane[:].bitcast(I32), 0)
    for quadrant in range(4):
        nc.sync.dma_start(
            out=plane[32 * quadrant : 32 * quadrant + 4].bitcast(I32),
            in_=scales[:, 4 * quadrant : 4 * quadrant + 4, :].rearrange("g r n -> r g n").bitcast(I32),
        )
    return codes, plane


def transpose_words(nc, bank, token_words, identity):
    for u in range(2):
        nc.tensor.transpose(bank[:, u, :], token_words[:, u:WORDS:2], identity[:])


def tile_synapsemodel_pa_t_kernel(
    tc, z, attention_out, Wz_words, Wz_scales, bz, gz, bz_ln, w1_deq_words, w1_deq_scales, b1, g1, b1_ln, out
):
    nc = tc.nc
    z_units = z.rearrange("(u p i) d -> u p i d", p=P, i=PAIR)
    attention_units = attention_out.rearrange("(u p i) h -> u p i h", p=P, i=PAIR)
    out_units = out.rearrange("(u p i) h -> u p i h", p=P, i=PAIR)

    with ExitStack() as stack:
        const = stack.enter_context(tc.tile_pool(name="const", bufs=1))
        brief = stack.enter_context(tc.tile_pool(name="brief", bufs=3))
        lasting = stack.enter_context(tc.tile_pool(name="lasting", bufs=5))
        psum = stack.enter_context(tc.psum_pool(name="psum", bufs=1))

        held = {}

        def load_z(u):
            z_rows = lasting.tile([P, PAIR, D], BF16, name="z_rows")
            nc.sync.dma_start(out=z_rows[:], in_=z_units[u])
            held["z_rows", u] = z_rows

        def load_attention(u):
            combined = lasting.tile([P, PAIR, 2 * H], BF16, name="combined")
            nc.sync.dma_start(out=combined[:, :, H : 2 * H], in_=attention_units[u])
            held["combined", u] = combined

        stack.enter_context(tc.manual_schedule())

        minus_half = const.tile([P, 2, PAIR], F32)
        nc.vector.memset(minus_half[:], -0.5)
        row_source = const.tile([P, len(ROW_VECTORS), H], BF16)
        nc.vector.memset(row_source[:], 0.0)
        column_source = const.tile([P, P], BF16)
        nc.vector.memset(column_source[:], 0.0)
        ones = const.tile([P, P], BF16)
        nc.vector.memset(ones[:], 1.0)

        table_loader = const.tile([P, 1], F32)
        nc.scalar.activation(out=table_loader[:], in_=minus_half[:, 0, 0:1], func=ACT.Gelu)

        identity = const.tile([P, P], F32)
        make_identity(nc, identity[:])

        load_z(0)
        given = {"bz": bz, "gz": gz, "bz_ln": bz_ln, "b1": b1}
        for j, name in enumerate(ROW_VECTORS):
            nc.sync.dma_start(out=row_source[0:1, j, :], in_=given[name].unsqueeze(0))
        load_z(1)
        wz_codes, wz_scales = load_weight(nc, const, Wz_words, Wz_scales, Z_PASSES, "wz")
        load_z(2)
        nc.sync.dma_start(out=column_source[0:HALVES, :], in_=g1.rearrange("(h f) -> h f", h=HALVES))
        nc.sync.dma_start(out=column_source[HALVES : 2 * HALVES, :], in_=b1_ln.rearrange("(h f) -> h f", h=HALVES))
        w1_codes, w1_scales = load_weight(nc, const, w1_deq_words, w1_deq_scales, 1, "w1")

        rows = const.tile([P, SBUF_ROWS, H], F32)
        ln1_rows = psum.tile([P, PAIR, H], F32, name="ln1_rows")
        columns = const.tile([P, 2 * HALVES], F32)
        row_of = {"bz": rows[:, 0, :], "b1": rows[:, 1, :], "gz": ln1_rows[:, 0, :], "bz_ln": ln1_rows[:, 1, :]}
        bias_row = {1: row_of["bz"], 2: row_of["b1"]}
        g1_columns = columns[:, 0:HALVES]
        b1_ln_columns = columns[:, HALVES : 2 * HALVES]

        def spread_rows():
            row_bank = psum.tile([P, PAIR, H], F32, name="y1_bank")
            for first, bank in ((0, row_bank), (SBUF_ROWS, ln1_rows)):
                nc.tensor.matmul(
                    out=bank[:].rearrange("p j h -> p (j h)"),
                    lhsT=ones[:],
                    rhs=row_source[:, first : first + PAIR, :].rearrange("p j h -> p (j h)"),
                    start=True,
                    stop=True,
                )
            nc.scalar.copy(out=rows[:], in_=row_bank[:])
        def spread_columns():
            column_source_f32 = const.tile([P, P], F32)
            nc.vector.tensor_copy(out=column_source_f32[:], in_=column_source[:])
            column_bank = psum.tile([P, PAIR, H], F32, name="token_bank")
            nc.tensor.transpose(column_bank[:, 0, 0:P], column_source_f32[:], identity[:])
            held["column_bank"] = column_bank

        def copy_columns():
            nc.vector.tensor_copy(out=columns[:], in_=held["column_bank"][:, 0, 0 : 2 * HALVES])

        def transpose_z(u):
            z_words = held["z_rows", u][:].bitcast(F32)
            z_grouped = lasting.tile([P, PAIR, Z_PASSES, P, PACK], BF16, name="z_grouped", align_bytes=64)
            for i in range(PAIR):
                z_bank = psum.tile([P, Z_PASSES, 2, P], F32, name="z_bank", bufs=Z_BANKS)
                for g in range(Z_PASSES):
                    transpose_words(nc, z_bank[:, g], z_words[:, i, WORDS * g : WORDS * (g + 1)], identity)
                nc.scalar.copy(out=z_grouped[:, i].bitcast(F32), in_=z_bank[:].rearrange("p g u r -> p g r u"))
            held["z_grouped", u] = z_grouped

        def quantise_z(u):
            z_codes = brief.tile([P, PAIR, Z_PASSES, P], U32, name="z_codes", align_bytes=64)
            z_scales = brief.tile([P, PAIR, Z_PASSES, P], U8, name="z_scales", align_bytes=64)
            nc.vector.quantize_mx(
                out=z_codes[:].rearrange("p i g r -> p (i g r)").bitcast(FP8X4),
                scales=z_scales[:].rearrange("p i g r -> p (i g r)"),
                in_=held["z_grouped", u][:].rearrange("p i g r t -> p (i g r t)"),
            )
            held["z_codes", u] = z_codes
            held["z_scales", u] = z_scales

        def multiply_z(u):
            z_codes, z_scales = held["z_codes", u], held["z_scales", u]
            y_bank = psum.tile([P, PAIR, H], F32, name="y1_bank")
            for i in range(PAIR):
                for g in range(Z_PASSES):
                    nc.tensor.matmul_mx(
                        out=y_bank[:, i, :],
                        lhsT=z_codes[:, i, g, :].bitcast(FP8X4),
                        lhsT_scale=z_scales[:, i, g, :],
                        rhs=wz_codes[:, g, :].bitcast(FP8X4),
                        rhs_scale=wz_scales[:, g, :],
                        start=(g == 0),
                        stop=(g == Z_PASSES - 1),
                    )
            held["y_bank", 1, u] = y_bank

        def layers_of_step(t):
            live = [layer - 1 for layer in (1, 2) if 0 <= t - BIAS_LAG[layer] < UNITS]
            return slice(live[0], live[-1] + 1) if live else None

        def statistics_engine(layers):
            return nc.gpsimd if layers.start == 0 else nc.vector

        def add_bias(layer, u):
            t = u + BIAS_LAG[layer]
            if ("row_sum", t) not in held:
                held["row_sum", t] = lasting.tile([P, 2, PAIR], F32, name="row_sum")
            y_bank = held["y_bank", layer, u]
            x = lasting.tile([P, PAIR, H], F32, name="x%d" % layer)
            for i in range(PAIR):
                nc.vector.scalar_tensor_tensor(
                    out=x[:, i, :],
                    in0=y_bank[:, i, :],
                    scalar=1.0,
                    in1=bias_row[layer],
                    op0=ALU.mult,
                    op1=ALU.add,
                    accum_out=held["row_sum", t][:, layer - 1, i : i + 1],
                )
            held["x", layer, u] = x

        def means(t):
            layers = layers_of_step(t)
            if layers is not None:
                neg_mean = lasting.tile([P, 2, PAIR], F32, name="neg_mean")
                statistics_engine(layers).tensor_scalar(
                    out=neg_mean[:, layers], in0=held["row_sum", t][:, layers],
                    scalar1=-1.0 / H, scalar2=0.0, op0=ALU.mult, op1=ALU.add,
                )
                held["neg_mean", t] = neg_mean
                held["square_sum", t] = lasting.tile([P, 2, PAIR], F32, name="square_sum")

        def sum_squares(layer, u):
            t = u + BIAS_LAG[layer]
            for i in range(PAIR):
                squares = lasting.tile([P, H], BF16, name="squares", bufs=SQUARE_BUFS)
                nc.scalar.activation(
                    out=squares[:],
                    in_=held["x", layer, u][:, i, :],
                    func=ACT.Square,
                    bias=held["row_sum", t][:, layer - 1, i : i + 1],
                    scale=-1.0 * H,
                    accum_out=held["square_sum", t][:, layer - 1, i : i + 1],
                )

        def normalised_on_gpsimd(u):
            return 0 <= u < UNITS and u + NORMALISE_LAG < UNITS + PROJECT_LAG

        def deviations(t):
            layers = layers_of_step(t)
            if layers is not None:
                variance_eps = lasting.tile([P, 2, PAIR], F32, name="variance_eps")
                statistics_engine(layers).tensor_scalar(
                    out=variance_eps[:, layers], in0=held["square_sum", t][:, layers],
                    scalar1=1.0 / (H * H * H), scalar2=LN_EPS, op0=ALU.mult, op1=ALU.add,
                )
                rstd = lasting.tile([P, 2, PAIR], F32, name="rstd")
                nc.gpsimd.tensor_tensor(
                    out=rstd[:, layers], in0=variance_eps[:, layers], in1=minus_half[:, layers], op=ALU.pow
                )
                held["rstd", t] = rstd
                if normalised_on_gpsimd(t - BIAS_LAG[2]):
                    shift = lasting.tile([P, PAIR], F32, name="shift")
                    nc.gpsimd.tensor_tensor(out=shift[:], in0=held["neg_mean", t][:, 1], in1=rstd[:, 1], op=ALU.mult)
                    held["shift", t] = shift

        def centre(u):
            neg_mean = held["neg_mean", u + BIAS_LAG[1]]
            centred = brief.tile([P, PAIR, H], F32, name="centred")
            for i in range(PAIR):
                nc.vector.scalar_tensor_tensor(
                    out=centred[:, i, :], in0=held["x", 1, u][:, i, :],
                    scalar=neg_mean[:, 0, i : i + 1], in1=row_of["gz"],
                    op0=ALU.add, op1=ALU.mult,
                )
            held["centred", u] = centred

        def project(u):
            rstd = held["rstd", u + BIAS_LAG[1]]
            for i in range(PAIR):
                nc.vector.scalar_tensor_tensor(
                    out=held["combined", u][:, i, 0:H], in0=held["centred", u][:, i, :],
                    scalar=rstd[:, 0, i : i + 1], in1=row_of["bz_ln"],
                    op0=ALU.mult, op1=ALU.add,
                )

        def transpose_combined(u):
            combined_words = held["combined", u][:].bitcast(F32)
            c_bank = psum.tile([P, PAIR, 2, P], F32, name="c_bank")
            for i in range(PAIR):
                transpose_words(nc, c_bank[:, i], combined_words[:, i, :], identity)
            c_grouped = brief.tile([P, PAIR, P, PACK], BF16, name="c_grouped", align_bytes=64)
            nc.scalar.copy(out=c_grouped[:].bitcast(F32), in_=c_bank[:].rearrange("p i u r -> p i r u"))
            held["c_grouped", u] = c_grouped

        def quantise_combined(u):
            c_codes = brief.tile([P, PAIR, P], U32, name="c_codes", align_bytes=64)
            c_scales = brief.tile([P, PAIR, P], U8, name="c_scales", align_bytes=64)
            nc.vector.quantize_mx(
                out=c_codes[:].rearrange("p i r -> p (i r)").bitcast(FP8X4),
                scales=c_scales[:].rearrange("p i r -> p (i r)"),
                in_=held["c_grouped", u][:].rearrange("p i r t -> p (i r t)"),
            )
            held["c_codes", u] = c_codes
            held["c_scales", u] = c_scales

        def multiply_combined(u):
            c_codes, c_scales = held["c_codes", u], held["c_scales", u]
            y_bank = psum.tile([P, PAIR, H], F32, name="y2_bank")
            for i in range(PAIR):
                nc.tensor.matmul_mx(
                    out=y_bank[:, i, :],
                    lhsT=c_codes[:, i, :].bitcast(FP8X4),
                    lhsT_scale=c_scales[:, i, :],
                    rhs=w1_codes[:, 0, :].bitcast(FP8X4),
                    rhs_scale=w1_scales[:, 0, :],
                    start=True,
                    stop=True,
                )
            held["y_bank", 2, u] = y_bank

        def normalise(u):
            t = u + BIAS_LAG[2]
            normed = brief.tile([P, PAIR, H], F32, name="normed")
            for i in range(PAIR):
                x = held["x", 2, u][:, i, :]
                rstd = held["rstd", t][:, 1, i : i + 1]
                if normalised_on_gpsimd(u):
                    nc.gpsimd.tensor_scalar(
                        out=normed[:, i, :], in0=x, scalar1=rstd, scalar2=held["shift", t][:, i : i + 1],
                        op0=ALU.mult, op1=ALU.add,
                    )
                else:
                    nc.vector.tensor_scalar(
                        out=normed[:, i, :], in0=x, scalar1=held["neg_mean", t][:, 1, i : i + 1], scalar2=rstd,
                        op0=ALU.add, op1=ALU.mult,
                    )
            held["normed", u] = normed

        def gelu_by_feature(u):
            feature_bank = psum.tile([P, HALVES, PAIR, P], F32, name="feature_bank")
            for h in range(HALVES):
                for i in range(PAIR):
                    nc.tensor.transpose(feature_bank[:, h, i, :], held["normed", u][:, i, P * h : P * (h + 1)], identity[:])
            activated = brief.tile([P, HALVES, PAIR, P], F32, name="activated")
            for h in range(HALVES):
                nc.scalar.activation(
                    out=activated[:, h].rearrange("p i r -> p (i r)"),
                    in_=feature_bank[:, h].rearrange("p i r -> p (i r)"),
                    func=ACT.Gelu,
                    bias=b1_ln_columns[:, h : h + 1],
                    scale=g1_columns[:, h : h + 1],
                )
            held["activated", u] = activated

        def store_by_token(u):
            token_bank = psum.tile([P, PAIR, H], F32, name="token_bank")
            for i in range(PAIR):
                for h in range(HALVES):
                    nc.tensor.transpose(token_bank[:, i, P * h : P * (h + 1)], held["activated", u][:, h, i, :], identity[:])
            result = brief.tile([P, PAIR, H], F32, name="result", bufs=UNITS)
            if u % 5 in (1, 3):
                nc.vector.tensor_copy(out=result[:], in_=token_bank[:])
            else:
                nc.scalar.copy(out=result[:], in_=token_bank[:])
            nc.sync.dma_start(out=out_units[u], in_=result[:])

        def run(stage, *unit):
            if 0 <= unit[-1] < UNITS:
                stage(*unit)

        def step(s):
            run(load_z, s + LOAD_AHEAD)
            run(load_attention, s - 3)
            run(normalise, s - NORMALISE_LAG)
            run(quantise_z, s - 2)
            run(quantise_combined, s - 7)
            run(multiply_z, s - 3)
            run(multiply_combined, s - 8)
            run(add_bias, 1, s - BIAS_LAG[1])
            run(add_bias, 2, s - BIAS_LAG[2])
            run(centre, s - 4)
            run(sum_squares, 1, s - 4)
            run(sum_squares, 2, s - 9)
            deviations(s - 1)
            run(project, s - PROJECT_LAG)
            run(transpose_combined, s - 6)
            run(gelu_by_feature, s - 12)
            run(store_by_token, s - LAST_LAG)
            run(transpose_z, s)
            means(s)

        for s in range(UNITS + LAST_LAG + 1):
            if s == FIRST_ROW_STEP - 1:
                spread_rows()
            if s == FIRST_COLUMN_STEP:
                spread_columns()
            if s == FIRST_COLUMN_STEP + 2:
                copy_columns()
            step(s)
